import numpy as np
import ml_dtypes


def mxq(x, axis, fmt="e4m3"):
    dtype, down = {"e4m3": (ml_dtypes.float8_e4m3fn, 7), "e5m2": (ml_dtypes.float8_e5m2, 14)}[fmt]
    v = np.moveaxis(np.asarray(x, np.float32).astype(ml_dtypes.bfloat16).astype(np.float64), axis, -1)
    blocks = v.reshape(v.shape[:-1] + (-1, 32))
    amax = np.abs(blocks).max(-1, keepdims=True)
    byte = np.maximum(np.where(amax > 0, np.frexp(amax)[1] - 1 + 127, 0) - down, 1)
    scale = np.exp2(byte - 127.0)
    codes = (blocks / scale).astype(np.float32).astype(dtype).astype(np.float64)
    return np.moveaxis((codes * scale).reshape(v.shape), -1, axis)


WIDE = False


def mx_kscale(k):
    if not WIDE:
        return np.ones(k)
    levels = np.array([10, -10, 5, -5, 0])
    a = np.random.permutation(np.resize(levels, k // 512 * 4)).reshape(k // 512, 4)
    idx = np.arange(k)
    return np.exp2(a[idx // 512, idx % 128 // 32])


BF16 = ml_dtypes.bfloat16


def bf(x):
    return np.asarray(x, np.float32).astype(BF16)


def f64(x):
    return np.asarray(x).astype(np.float64)


B, C, H, W = 4, 512, 32, 32
GAMMA_INIT = 0.1


def setup_inputs():
    t = np.exp2(np.round(np.log2(mx_kscale(C)) / 2))
    gain = np.exp(0.5 * np.random.standard_normal((B, 1, H, W)))
    x = np.random.standard_normal((B, C, H, W)) * gain * t[None, :, None, None]
    gamma = (GAMMA_INIT * np.eye(C) + np.abs(np.random.standard_normal((C, C))) / C) / (t * t)[None, :]
    beta = 0.5 + np.random.random(C)
    return {"x": bf(x), "gamma": bf(gamma), "beta": bf(beta)}


def reference(x, gamma, beta):
    xf = f64(x)
    sq = (xf * xf).reshape(B, C, H * W)
    norm = (mxq(f64(gamma), 1, "e4m3") @ mxq(sq, 1, "e4m3")) + f64(beta)[None, :, None]
    return xf / np.sqrt(norm.reshape(B, C, H, W))

@@ -1,0 +1,152 @@
+from contextlib import ExitStack
+
+import concourse.mybir as mybir
+from concourse.masks import make_identity
+
+F32 = mybir.dt.float32
+BF16 = mybir.dt.bfloat16
+U32 = mybir.dt.uint32
+U8 = mybir.dt.uint8
+FP8X4 = mybir.dt.float8_e4m3fn_x4
+ACT = mybir.ActivationFunctionType
+ALU = mybir.AluOpType
+
+B, C, HW = 4, 512, 1024
+P = 128
+PACK = 4
+NPIX = 512
+UNITS = B * HW // NPIX
+FLOPS = 2 * B * C * C * HW
+
+MANUAL = True
+WS = 320
+
+
+def tile_gdn_kernel(tc, x, gamma, beta, out):
+    nc = tc.nc
+    xv = x.rearrange("b (p j) h w -> b p j (h w)", j=PACK)
+    ov = out.rearrange("b (p j) h w -> b p j (h w)", j=PACK)
+    gv = gamma.rearrange("(p j) c -> p j c", j=PACK)
+    bv = beta.rearrange("(p j) -> p j", j=PACK)
+
+    with ExitStack() as ctx:
+        if MANUAL:
+            ctx.enter_context(tc.manual_schedule())
+        const = ctx.enter_context(tc.tile_pool(name="const", bufs=1))
+        grp_pool = ctx.enter_context(tc.tile_pool(name="grp", bufs=4))
+        q_pool = ctx.enter_context(tc.tile_pool(name="q", bufs=4))
+        r_pool = ctx.enter_context(tc.tile_pool(name="r", bufs=8))
+        o_pool = ctx.enter_context(tc.tile_pool(name="o", bufs=4))
+        psum = ctx.enter_context(tc.psum_pool(name="psum", bufs=8))
+
+        g_sb = const.tile([P, PACK, C], BF16, name="g_sb")
+        nc.sync.dma_start(out=g_sb[:], in_=gv)
+        x_sb = [const.tile([P, PACK, HW], BF16, name="x%d" % b) for b in range(B)]
+        nc.sync.dma_start(out=x_sb[0][:, :, 0:NPIX], in_=xv[0][:, :, 0:NPIX])
+        nc.sync.dma_start(out=x_sb[0][:, :, NPIX:HW], in_=xv[0][:, :, NPIX:HW])
+        for b in range(1, B):
+            nc.sync.dma_start(out=x_sb[b][:], in_=xv[b])
+        beta_bf = const.tile([P, PACK], BF16, name="beta_bf")
+        nc.scalar.dma_start(out=beta_bf[:], in_=bv)
+
+        warm_in = const.tile([P, 1], F32, name="warm_in")
+        warm_out = const.tile([P, 1], F32, name="warm_out")
+        nc.vector.memset(warm_in[:], 1.0)
+        nc.scalar.activation(out=warm_out[:], in_=warm_in[:], func=ACT.Abs_reciprocal_sqrt)
+
+        ident = const.tile([P, P], F32, name="ident")
+        make_identity(nc, ident[:])
+        beta_f = const.tile([P, PACK], F32, name="beta_f")
+        nc.gpsimd.tensor_copy(out=beta_f[:], in_=beta_bf[:])
+
+        grp = {}
+        codes = {}
+        scales = {}
+        acc = {}
+
+        def x_unit(u):
+            b, h = divmod(u, HW // NPIX)
+            return x_sb[b][:, :, h * NPIX:(h + 1) * NPIX]
+
+        def squares(u):
+            grp[u] = grp_pool.tile([P, NPIX, PACK], BF16, name="grp", align_bytes=64)
+            src = x_unit(u)
+            nc.scalar.activation(
+                out=grp[u][:, 0:WS, :].rearrange("p (c i) t -> p c t i", i=4),
+                in_=src[:, :, 0:WS].rearrange("p t (c i) -> p c t i", i=4),
+                func=ACT.Square,
+            )
+            sv = src[:, :, WS:NPIX].rearrange("p t w -> p w t")
+            nc.vector.tensor_tensor(out=grp[u][:, WS:NPIX, :], in0=sv, in1=sv, op=ALU.mult)
+
+        def quantise(u):
+            codes[u] = q_pool.tile([P, NPIX], U32, name="codes", align_bytes=64)
+            scales[u] = q_pool.tile([P, NPIX], U8, name="scales", align_bytes=64)
+            nc.vector.quantize_mx(
+                out=codes[u][:].bitcast(FP8X4),
+                scales=scales[u][:],
+                in_=grp[u][:].rearrange("p w t -> p (w t)"),
+            )
+
+        def passes(u):
+            for j in range(PACK):
+                acc[u, j] = psum.tile([P, NPIX], F32, name="bank")
+                nc.tensor.matmul_mx(
+                    out=acc[u, j][:],
+                    lhsT=g_codes[:, j * P:(j + 1) * P].bitcast(FP8X4),
+                    lhsT_scale=g_scales[:, j * P:(j + 1) * P],
+                    rhs=codes[u][:].bitcast(FP8X4),
+                    rhs_scale=scales[u][:],
+                    start=True,
+                    stop=True,
+                )
+
+        def finish(u):
+            b, h = divmod(u, HW // NPIX)
+            o_sb = o_pool.tile([P, PACK, NPIX], F32, name="o_sb")
+            src = x_unit(u)
+            for j in range(PACK):
+                r_sb = r_pool.tile([P, NPIX], F32, name="r_sb")
+                nc.scalar.activation(
+                    out=r_sb[:], in_=acc[u, j][:], func=ACT.Abs_reciprocal_sqrt,
+                    bias=beta_f[:, j:j + 1], scale=1.0,
+                )
+                nc.vector.tensor_tensor(out=o_sb[:, j, :], in0=src[:, j, :], in1=r_sb[:], op=ALU.mult)
+                if u == UNITS - 1:
+                    nc.sync.dma_start(out=ov[b][:, j, h * NPIX:(h + 1) * NPIX], in_=o_sb[:, j, :])
+            if u != UNITS - 1:
+                nc.sync.dma_start(out=ov[b][:, :, h * NPIX:(h + 1) * NPIX], in_=o_sb[:])
+
+        g_words = g_sb[:].bitcast(F32).rearrange("p j (q u) -> p j q u", u=2)
+        g_grp = const.tile([P, PACK, P, PACK], BF16, name="g_grp", align_bytes=64)
+        g_grp_words = g_grp[:].bitcast(F32)
+        g_codes = const.tile([P, C], U32, name="g_codes", align_bytes=64)
+        g_scales = const.tile([P, C], U8, name="g_scales", align_bytes=64)
+        g_t = []
+        for half in range(2):
+            g_t.append(psum.tile([P, 4, P], F32, name="bank"))
+            for jj in range(2):
+                for u in range(2):
+                    nc.tensor.transpose(g_t[half][:, 2 * jj + u, :], g_words[:, 2 * half + jj, :, u], ident[:])
+
+        squares(0)
+        for half in range(2):
+            nc.vector.tensor_copy(
+                out=g_grp_words[:, 2 * half:2 * half + 2, :, :],
+                in_=g_t[half][:].rearrange("p (jj u) o -> p jj o u", u=2),
+            )
+        squares(1)
+        nc.vector.quantize_mx(
+            out=g_codes[:].bitcast(FP8X4),
+            scales=g_scales[:],
+            in_=g_grp[:].rearrange("p j o t -> p (j o t)"),
+        )
+        quantise(0)
+        passes(0)
+        for i in range(UNITS):
+            if i + 1 < UNITS:
+                quantise(i + 1)
+                passes(i + 1)
+            if i + 2 < UNITS:
+                squares(i + 2)
+            finish(i)

@@ -15,11 +15,16 @@ B, C, HW = 4, 512, 1024
 P = 128
 PACK = 4
 NPIX = 512
-UNITS = B * HW // NPIX
+HALVES = HW // NPIX
+UNITS = B * HALVES
 FLOPS = 2 * B * C * C * HW
 
 MANUAL = True
-WS = 320
+WS = (256, 320, 256, 336, 336, 336, 336, 336)
+MULG = (1, 1, 1, 1, 1, 1, 1, 1)
+STG = (2, 2, 2, 2, 2, 2, 1, 1)
+VFORM = "perm"
+TAIL = 2
 
 
 def tile_gdn_kernel(tc, x, gamma, beta, out):
@@ -35,15 +40,17 @@ def tile_gdn_kernel(tc, x, gamma, beta, out):
         const = ctx.enter_context(tc.tile_pool(name="const", bufs=1))
         grp_pool = ctx.enter_context(tc.tile_pool(name="grp", bufs=4))
         q_pool = ctx.enter_context(tc.tile_pool(name="q", bufs=4))
-        r_pool = ctx.enter_context(tc.tile_pool(name="r", bufs=8))
+        r_pool = ctx.enter_context(tc.tile_pool(name="r", bufs=6))
         o_pool = ctx.enter_context(tc.tile_pool(name="o", bufs=4))
         psum = ctx.enter_context(tc.psum_pool(name="psum", bufs=8))
 
+        x0_sb = [const.tile([P, PACK, NPIX], BF16, name="x0%d" % h) for h in range(HALVES)]
+        x_sb = [None] + [const.tile([P, PACK, HW], BF16, name="x%d" % b) for b in range(1, B)]
         g_sb = const.tile([P, PACK, C], BF16, name="g_sb")
-        nc.sync.dma_start(out=g_sb[:], in_=gv)
-        x_sb = [const.tile([P, PACK, HW], BF16, name="x%d" % b) for b in range(B)]
-        nc.sync.dma_start(out=x_sb[0][:, :, 0:NPIX], in_=xv[0][:, :, 0:NPIX])
-        nc.sync.dma_start(out=x_sb[0][:, :, NPIX:HW], in_=xv[0][:, :, NPIX:HW])
+        nc.sync.dma_start(out=g_sb[:, 0:2, :], in_=gv[:, 0:2, :])
+        nc.sync.dma_start(out=x0_sb[0][:], in_=xv[0][:, :, 0:NPIX])
+        nc.sync.dma_start(out=g_sb[:, 2:4, :], in_=gv[:, 2:4, :])
+        nc.sync.dma_start(out=x0_sb[1][:], in_=xv[0][:, :, NPIX:HW])
         for b in range(1, B):
             nc.sync.dma_start(out=x_sb[b][:], in_=xv[b])
         beta_bf = const.tile([P, PACK], BF16, name="beta_bf")
@@ -65,19 +72,27 @@ def tile_gdn_kernel(tc, x, gamma, beta, out):
         acc = {}
 
         def x_unit(u):
-            b, h = divmod(u, HW // NPIX)
+            b, h = divmod(u, HALVES)
+            if b == 0:
+                return x0_sb[h][:]
             return x_sb[b][:, :, h * NPIX:(h + 1) * NPIX]
 
         def squares(u):
+            ws = WS[u]
             grp[u] = grp_pool.tile([P, NPIX, PACK], BF16, name="grp", align_bytes=64)
             src = x_unit(u)
             nc.scalar.activation(
-                out=grp[u][:, 0:WS, :].rearrange("p (c i) t -> p c t i", i=4),
-                in_=src[:, :, 0:WS].rearrange("p t (c i) -> p c t i", i=4),
+                out=grp[u][:, 0:ws, :].rearrange("p (c i) t -> p c t i", i=4),
+                in_=src[:, :, 0:ws].rearrange("p t (c i) -> p c t i", i=4),
                 func=ACT.Square,
             )
-            sv = src[:, :, WS:NPIX].rearrange("p t w -> p w t")
-            nc.vector.tensor_tensor(out=grp[u][:, WS:NPIX, :], in0=sv, in1=sv, op=ALU.mult)
+            if VFORM == "perm":
+                sv = src[:, :, ws:NPIX].rearrange("p t w -> p w t")
+                dv = grp[u][:, ws:NPIX, :]
+            else:
+                sv = src[:, :, ws:NPIX].rearrange("p t (c i) -> p c t i", i=4)
+                dv = grp[u][:, ws:NPIX, :].rearrange("p (c i) t -> p c t i", i=4)
+            nc.vector.tensor_tensor(out=dv, in0=sv, in1=sv, op=ALU.mult)
 
         def quantise(u):
             codes[u] = q_pool.tile([P, NPIX], U32, name="codes", align_bytes=64)
@@ -102,20 +117,36 @@ def tile_gdn_kernel(tc, x, gamma, beta, out):
                 )
 
         def finish(u):
-            b, h = divmod(u, HW // NPIX)
-            o_sb = o_pool.tile([P, PACK, NPIX], F32, name="o_sb")
+            b, h = divmod(u, HALVES)
+            mg, sg = MULG[u], STG[u]
             src = x_unit(u)
+            o_sb = o_pool.tile([P, PACK, NPIX], F32, name="o_sb")
+            r_sb = None
             for j in range(PACK):
-                r_sb = r_pool.tile([P, NPIX], F32, name="r_sb")
+                if u == UNITS - 1 and j == PACK - 1 and TAIL > 1:
+                    r_sb = r_pool.tile([P, 1, NPIX], F32, name="r_sb")
+                    w = NPIX // TAIL
+                    for k in range(TAIL):
+                        cols = slice(k * w, (k + 1) * w)
+                        nc.scalar.activation(
+                            out=r_sb[:, 0, cols], in_=acc[u, j][:, cols], func=ACT.Abs_reciprocal_sqrt,
+                            bias=beta_f[:, j:j + 1], scale=1.0,
+                        )
+                        nc.vector.tensor_tensor(out=o_sb[:, j, cols], in0=src[:, j, cols], in1=r_sb[:, 0, cols], op=ALU.mult)
+                        nc.sync.dma_start(out=ov[b][:, j, h * NPIX + k * w:h * NPIX + (k + 1) * w], in_=o_sb[:, j, cols])
+                    continue
+                if j % mg == 0:
+                    r_sb = r_pool.tile([P, mg, NPIX], F32, name="r_sb")
                 nc.scalar.activation(
-                    out=r_sb[:], in_=acc[u, j][:], func=ACT.Abs_reciprocal_sqrt,
+                    out=r_sb[:, j % mg, :], in_=acc[u, j][:], func=ACT.Abs_reciprocal_sqrt,
                     bias=beta_f[:, j:j + 1], scale=1.0,
                 )
-                nc.vector.tensor_tensor(out=o_sb[:, j, :], in0=src[:, j, :], in1=r_sb[:], op=ALU.mult)
-                if u == UNITS - 1:
-                    nc.sync.dma_start(out=ov[b][:, j, h * NPIX:(h + 1) * NPIX], in_=o_sb[:, j, :])
-            if u != UNITS - 1:
-                nc.sync.dma_start(out=ov[b][:, :, h * NPIX:(h + 1) * NPIX], in_=o_sb[:])
+                if (j + 1) % mg == 0:
+                    js = slice(j + 1 - mg, j + 1)
+                    nc.vector.tensor_tensor(out=o_sb[:, js, :], in0=src[:, js, :], in1=r_sb[:], op=ALU.mult)
+                if (j + 1) % sg == 0:
+                    js = slice(j + 1 - sg, j + 1)
+                    nc.sync.dma_start(out=ov[b][:, js, h * NPIX:(h + 1) * NPIX], in_=o_sb[:, js, :])
 
         g_words = g_sb[:].bitcast(F32).rearrange("p j (q u) -> p j q u", u=2)
         g_grp = const.tile([P, PACK, P, PACK], BF16, name="g_grp", align_bytes=64)
@@ -123,25 +154,38 @@ def tile_gdn_kernel(tc, x, gamma, beta, out):
         g_codes = const.tile([P, C], U32, name="g_codes", align_bytes=64)
         g_scales = const.tile([P, C], U8, name="g_scales", align_bytes=64)
         g_t = []
-        for half in range(2):
+
+        def g_transposes(half):
             g_t.append(psum.tile([P, 4, P], F32, name="bank"))
             for jj in range(2):
                 for u in range(2):
                     nc.tensor.transpose(g_t[half][:, 2 * jj + u, :], g_words[:, 2 * half + jj, :, u], ident[:])
 
-        squares(0)
-        for half in range(2):
-            nc.vector.tensor_copy(
-                out=g_grp_words[:, 2 * half:2 * half + 2, :, :],
-                in_=g_t[half][:].rearrange("p (jj u) o -> p jj o u", u=2),
+        def g_copy(half, on_scalar):
+            dst = g_grp_words[:, 2 * half:2 * half + 2, :, :]
+            src = g_t[half][:].rearrange("p (jj u) o -> p jj o u", u=2)
+            if on_scalar:
+                nc.scalar.copy(out=dst, in_=src)
+            else:
+                nc.vector.tensor_copy(out=dst, in_=src)
+
+        def g_quantise(half):
+            cols = slice(half * 2 * P, (half + 1) * 2 * P)
+            nc.vector.quantize_mx(
+                out=g_codes[:, cols].bitcast(FP8X4),
+                scales=g_scales[:, cols],
+                in_=g_grp[:, 2 * half:2 * half + 2, :, :].rearrange("p j o t -> p (j o t)"),
             )
-        squares(1)
-        nc.vector.quantize_mx(
-            out=g_codes[:].bitcast(FP8X4),
-            scales=g_scales[:],
-            in_=g_grp[:].rearrange("p j o t -> p (j o t)"),
-        )
+
+        squares(0)
+        g_transposes(0)
+        g_transposes(1)
         quantise(0)
+        g_copy(0, True)
+        g_quantise(0)
+        squares(1)
+        g_copy(1, False)
+        g_quantise(1)
         passes(0)
         for i in range(UNITS):
             if i + 1 < UNITS:

@@ -25,6 +25,7 @@ MULG = (1, 1, 1, 1, 1, 1, 1, 1)
 STG = (2, 2, 2, 2, 2, 2, 1, 1)
 VFORM = "perm"
 TAIL = 2
+EARLY = (2, 0, 0, 0, 0, 0, 0, 0)
 
 
 def tile_gdn_kernel(tc, x, gamma, beta, out):
@@ -116,13 +117,17 @@ def tile_gdn_kernel(tc, x, gamma, beta, out):
                     stop=True,
                 )
 
-        def finish(u):
+        o_tiles = {}
+
+        def finish(u, j_list):
             b, h = divmod(u, HALVES)
             mg, sg = MULG[u], STG[u]
             src = x_unit(u)
-            o_sb = o_pool.tile([P, PACK, NPIX], F32, name="o_sb")
+            if j_list[0] == 0:
+                o_tiles[u] = o_pool.tile([P, PACK, NPIX], F32, name="o_sb")
+            o_sb = o_tiles[u]
             r_sb = None
-            for j in range(PACK):
+            for j in j_list:
                 if u == UNITS - 1 and j == PACK - 1 and TAIL > 1:
                     r_sb = r_pool.tile([P, 1, NPIX], F32, name="r_sb")
                     w = NPIX // TAIL
@@ -191,6 +196,9 @@ def tile_gdn_kernel(tc, x, gamma, beta, out):
             if i + 1 < UNITS:
                 quantise(i + 1)
                 passes(i + 1)
+            early = EARLY[i]
+            if early:
+                finish(i, list(range(early)))
             if i + 2 < UNITS:
                 squares(i + 2)
-            finish(i)
+            finish(i, list(range(early, PACK)))

@@ -20,7 +20,7 @@ UNITS = B * HALVES
 FLOPS = 2 * B * C * C * HW
 
 MANUAL = True
-WS = (256, 320, 256, 336, 336, 336, 336, 336)
+WS = (288, 352, 288, 368, 368, 368, 368, 368)
 MULG = (1, 1, 1, 1, 1, 1, 1, 1)
 STG = (2, 2, 2, 2, 2, 2, 1, 1)
 VFORM = "perm"

@@ -20,7 +20,7 @@ UNITS = B * HALVES
 FLOPS = 2 * B * C * C * HW
 
 MANUAL = True
-WS = (288, 352, 288, 368, 368, 368, 368, 368)
+WS = (272, 336, 272, 352, 352, 352, 352, 352)
 MULG = (1, 1, 1, 1, 1, 1, 1, 1)
 STG = (2, 2, 2, 2, 2, 2, 1, 1)
 VFORM = "perm"

@@ -25,7 +25,7 @@ MULG = (1, 1, 1, 1, 1, 1, 1, 1)
 STG = (2, 2, 2, 2, 2, 2, 1, 1)
 VFORM = "perm"
 TAIL = 2
-EARLY = (2, 0, 0, 0, 0, 0, 0, 0)
+EARLY = (0, 0, 0, 0, 0, 0, 0, 0)
 
 
 def tile_gdn_kernel(tc, x, gamma, beta, out):
@@ -45,14 +45,16 @@ def tile_gdn_kernel(tc, x, gamma, beta, out):
         o_pool = ctx.enter_context(tc.tile_pool(name="o", bufs=4))
         psum = ctx.enter_context(tc.psum_pool(name="psum", bufs=8))
 
-        x0_sb = [const.tile([P, PACK, NPIX], BF16, name="x0%d" % h) for h in range(HALVES)]
-        x_sb = [None] + [const.tile([P, PACK, HW], BF16, name="x%d" % b) for b in range(1, B)]
+        x0_sb = [const.tile([P, PACK, NPIX], BF16, name="x0%d" % h) for h in range(2 * HALVES)]
+        x_sb = [None, None] + [const.tile([P, PACK, HW], BF16, name="x%d" % b) for b in range(2, B)]
         g_sb = const.tile([P, PACK, C], BF16, name="g_sb")
         nc.sync.dma_start(out=g_sb[:, 0:2, :], in_=gv[:, 0:2, :])
         nc.sync.dma_start(out=x0_sb[0][:], in_=xv[0][:, :, 0:NPIX])
         nc.sync.dma_start(out=g_sb[:, 2:4, :], in_=gv[:, 2:4, :])
         nc.sync.dma_start(out=x0_sb[1][:], in_=xv[0][:, :, NPIX:HW])
-        for b in range(1, B):
+        for h in range(HALVES):
+            nc.sync.dma_start(out=x0_sb[HALVES + h][:], in_=xv[1][:, :, h * NPIX:(h + 1) * NPIX])
+        for b in range(2, B):
             nc.sync.dma_start(out=x_sb[b][:], in_=xv[b])
         beta_bf = const.tile([P, PACK], BF16, name="beta_bf")
         nc.scalar.dma_start(out=beta_bf[:], in_=bv)
@@ -74,8 +76,8 @@ def tile_gdn_kernel(tc, x, gamma, beta, out):
 
         def x_unit(u):
             b, h = divmod(u, HALVES)
-            if b == 0:
-                return x0_sb[h][:]
+            if b < 2:
+                return x0_sb[u][:]
             return x_sb[b][:, :, h * NPIX:(h + 1) * NPIX]
 
         def squares(u):

@@ -20,7 +20,7 @@ UNITS = B * HALVES
 FLOPS = 2 * B * C * C * HW
 
 MANUAL = True
-WS = (272, 336, 272, 352, 352, 352, 352, 352)
+WS = (272, 336, 272, 352, 352, 352, 352, 416)
 MULG = (1, 1, 1, 1, 1, 1, 1, 1)
 STG = (2, 2, 2, 2, 2, 2, 1, 1)
 VFORM = "perm"
@@ -80,15 +80,19 @@ def tile_gdn_kernel(tc, x, gamma, beta, out):
                 return x0_sb[u][:]
             return x_sb[b][:, :, h * NPIX:(h + 1) * NPIX]
 
-        def squares(u):
+        def squares_s(u):
             ws = WS[u]
-            grp[u] = grp_pool.tile([P, NPIX, PACK], BF16, name="grp", align_bytes=64)
             src = x_unit(u)
             nc.scalar.activation(
                 out=grp[u][:, 0:ws, :].rearrange("p (c i) t -> p c t i", i=4),
                 in_=src[:, :, 0:ws].rearrange("p t (c i) -> p c t i", i=4),
                 func=ACT.Square,
             )
+
+        def squares_v(u):
+            ws = WS[u]
+            grp[u] = grp_pool.tile([P, NPIX, PACK], BF16, name="grp", align_bytes=64)
+            src = x_unit(u)
             if VFORM == "perm":
                 sv = src[:, :, ws:NPIX].rearrange("p t w -> p w t")
                 dv = grp[u][:, ws:NPIX, :]
@@ -184,23 +188,29 @@ def tile_gdn_kernel(tc, x, gamma, beta, out):
                 in_=g_grp[:, 2 * half:2 * half + 2, :, :].rearrange("p j o t -> p (j o t)"),
             )
 
-        squares(0)
+        squares_v(0)
+        squares_s(0)
         g_transposes(0)
         g_transposes(1)
         quantise(0)
         g_copy(0, True)
         g_quantise(0)
-        squares(1)
+        squares_v(1)
+        squares_s(1)
         g_copy(1, False)
         g_quantise(1)
         passes(0)
+        last = UNITS - 1
         for i in range(UNITS):
-            if i + 1 < UNITS:
+            if i + 1 < last:
                 quantise(i + 1)
                 passes(i + 1)
-            early = EARLY[i]
-            if early:
-                finish(i, list(range(early)))
             if i + 2 < UNITS:
-                squares(i + 2)
-            finish(i, list(range(early, PACK)))
+                squares_v(i + 2)
+            if i + 2 < last:
+                squares_s(i + 2)
+            finish(i, list(range(PACK)))
+            if i + 2 == last:
+                squares_s(last)
+                quantise(last)
+                passes(last)

@@ -20,7 +20,7 @@ UNITS = B * HALVES
 FLOPS = 2 * B * C * C * HW
 
 MANUAL = True
-WS = (272, 336, 272, 352, 352, 352, 352, 416)
+WS = (256, 304, 304, 336, 336, 336, 336, 416)
 MULG = (1, 1, 1, 1, 1, 1, 1, 1)
 STG = (2, 2, 2, 2, 2, 2, 1, 1)
 VFORM = "perm"
@@ -49,7 +49,9 @@ def tile_gdn_kernel(tc, x, gamma, beta, out):
         x_sb = [None, None] + [const.tile([P, PACK, HW], BF16, name="x%d" % b) for b in range(2, B)]
         g_sb = const.tile([P, PACK, C], BF16, name="g_sb")
         nc.sync.dma_start(out=g_sb[:, 0:2, :], in_=gv[:, 0:2, :])
-        nc.sync.dma_start(out=x0_sb[0][:], in_=xv[0][:, :, 0:NPIX])
+        x00 = const.tile([P, 2, PACK, NPIX // 2], BF16, name="x00")
+        for a in range(2):
+            nc.sync.dma_start(out=x00[:, a, :, :], in_=xv[0][:, :, a * (NPIX // 2):(a + 1) * (NPIX // 2)])
         nc.sync.dma_start(out=g_sb[:, 2:4, :], in_=gv[:, 2:4, :])
         nc.sync.dma_start(out=x0_sb[1][:], in_=xv[0][:, :, NPIX:HW])
         for h in range(HALVES):
@@ -152,7 +154,11 @@ def tile_gdn_kernel(tc, x, gamma, beta, out):
                     out=r_sb[:, j % mg, :], in_=acc[u, j][:], func=ACT.Abs_reciprocal_sqrt,
                     bias=beta_f[:, j:j + 1], scale=1.0,
                 )
-                if (j + 1) % mg == 0:
+                if u == 0:
+                    nc.vector.tensor_tensor(
+                        out=o_sb[:, j, :].rearrange("p (a w) -> p a w", a=2), in0=x00[:, :, j, :],
+                        in1=r_sb[:, 0, :].rearrange("p (a w) -> p a w", a=2), op=ALU.mult)
+                elif (j + 1) % mg == 0:
                     js = slice(j + 1 - mg, j + 1)
                     nc.vector.tensor_tensor(out=o_sb[:, js, :], in0=src[:, js, :], in1=r_sb[:], op=ALU.mult)
                 if (j + 1) % sg == 0:
@@ -188,8 +194,17 @@ def tile_gdn_kernel(tc, x, gamma, beta, out):
                 in_=g_grp[:, 2 * half:2 * half + 2, :, :].rearrange("p j o t -> p (j o t)"),
             )
 
-        squares_v(0)
-        squares_s(0)
+        grp[0] = grp_pool.tile([P, NPIX, PACK], BF16, name="grp", align_bytes=64)
+        hp = NPIX // 2
+        w0 = WS[0] // 2
+        for a in range(2):
+            nc.scalar.activation(
+                out=grp[0][:, a * hp:a * hp + w0, :].rearrange("p (c i) t -> p c t i", i=4),
+                in_=x00[:, a, :, 0:w0].rearrange("p t (c i) -> p c t i", i=4),
+                func=ACT.Square,
+            )
+            sv0 = x00[:, a, :, w0:hp].rearrange("p t w -> p w t")
+            nc.vector.tensor_tensor(out=grp[0][:, a * hp + w0:(a + 1) * hp, :], in0=sv0, in1=sv0, op=ALU.mult)
         g_transposes(0)
         g_transposes(1)
         quantise(0)

@@ -20,7 +20,8 @@ UNITS = B * HALVES
 FLOPS = 2 * B * C * C * HW
 
 MANUAL = True
-WS = (256, 304, 304, 336, 336, 336, 336, 416)
+WS = (256, 352, 288, 336, 336, 336, 336, 448)
+SPLIT = ((128, 128), (256, 96))
 MULG = (1, 1, 1, 1, 1, 1, 1, 1)
 STG = (2, 2, 2, 2, 2, 2, 1, 1)
 VFORM = "perm"
@@ -49,11 +50,12 @@ def tile_gdn_kernel(tc, x, gamma, beta, out):
         x_sb = [None, None] + [const.tile([P, PACK, HW], BF16, name="x%d" % b) for b in range(2, B)]
         g_sb = const.tile([P, PACK, C], BF16, name="g_sb")
         nc.sync.dma_start(out=g_sb[:, 0:2, :], in_=gv[:, 0:2, :])
-        x00 = const.tile([P, 2, PACK, NPIX // 2], BF16, name="x00")
+        xp = [const.tile([P, 2, PACK, NPIX // 2], BF16, name="xp%d" % u) for u in range(2)]
         for a in range(2):
-            nc.sync.dma_start(out=x00[:, a, :, :], in_=xv[0][:, :, a * (NPIX // 2):(a + 1) * (NPIX // 2)])
+            nc.sync.dma_start(out=xp[0][:, a, :, :], in_=xv[0][:, :, a * (NPIX // 2):(a + 1) * (NPIX // 2)])
         nc.sync.dma_start(out=g_sb[:, 2:4, :], in_=gv[:, 2:4, :])
-        nc.sync.dma_start(out=x0_sb[1][:], in_=xv[0][:, :, NPIX:HW])
+        for a in range(2):
+            nc.sync.dma_start(out=xp[1][:, a, :, :], in_=xv[0][:, :, NPIX + a * (NPIX // 2):NPIX + (a + 1) * (NPIX // 2)])
         for h in range(HALVES):
             nc.sync.dma_start(out=x0_sb[HALVES + h][:], in_=xv[1][:, :, h * NPIX:(h + 1) * NPIX])
         for b in range(2, B):
@@ -154,9 +156,9 @@ def tile_gdn_kernel(tc, x, gamma, beta, out):
                     out=r_sb[:, j % mg, :], in_=acc[u, j][:], func=ACT.Abs_reciprocal_sqrt,
                     bias=beta_f[:, j:j + 1], scale=1.0,
                 )
-                if u == 0:
+                if u < 2:
                     nc.vector.tensor_tensor(
-                        out=o_sb[:, j, :].rearrange("p (a w) -> p a w", a=2), in0=x00[:, :, j, :],
+                        out=o_sb[:, j, :].rearrange("p (a w) -> p a w", a=2), in0=xp[u][:, :, j, :],
                         in1=r_sb[:, 0, :].rearrange("p (a w) -> p a w", a=2), op=ALU.mult)
                 elif (j + 1) % mg == 0:
                     js = slice(j + 1 - mg, j + 1)
@@ -194,24 +196,28 @@ def tile_gdn_kernel(tc, x, gamma, beta, out):
                 in_=g_grp[:, 2 * half:2 * half + 2, :, :].rearrange("p j o t -> p (j o t)"),
             )
 
-        grp[0] = grp_pool.tile([P, NPIX, PACK], BF16, name="grp", align_bytes=64)
         hp = NPIX // 2
-        w0 = WS[0] // 2
-        for a in range(2):
-            nc.scalar.activation(
-                out=grp[0][:, a * hp:a * hp + w0, :].rearrange("p (c i) t -> p c t i", i=4),
-                in_=x00[:, a, :, 0:w0].rearrange("p t (c i) -> p c t i", i=4),
-                func=ACT.Square,
-            )
-            sv0 = x00[:, a, :, w0:hp].rearrange("p t w -> p w t")
-            nc.vector.tensor_tensor(out=grp[0][:, a * hp + w0:(a + 1) * hp, :], in0=sv0, in1=sv0, op=ALU.mult)
+
+        def squares_pieces(u):
+            grp[u] = grp_pool.tile([P, NPIX, PACK], BF16, name="grp", align_bytes=64)
+            for a in range(2):
+                w0 = SPLIT[u][a]
+                nc.scalar.activation(
+                    out=grp[u][:, a * hp:a * hp + w0, :].rearrange("p (c i) t -> p c t i", i=4),
+                    in_=xp[u][:, a, :, 0:w0].rearrange("p t (c i) -> p c t i", i=4),
+                    func=ACT.Square,
+                )
+                if w0 < hp:
+                    sv0 = xp[u][:, a, :, w0:hp].rearrange("p t w -> p w t")
+                    nc.vector.tensor_tensor(out=grp[u][:, a * hp + w0:(a + 1) * hp, :], in0=sv0, in1=sv0, op=ALU.mult)
+
+        squares_pieces(0)
         g_transposes(0)
         g_transposes(1)
         quantise(0)
         g_copy(0, True)
         g_quantise(0)
-        squares_v(1)
-        squares_s(1)
+        squares_pieces(1)
         g_copy(1, False)
         g_quantise(1)
         passes(0)

@@ -219,11 +219,13 @@ def tile_gdn_kernel(tc, x, gamma, beta, out):
         g_quantise(0)
         squares_pieces(1)
         g_copy(1, False)
+        quantise(1)
         g_quantise(1)
         passes(0)
+        passes(1)
         last = UNITS - 1
         for i in range(UNITS):
-            if i + 1 < last:
+            if 0 < i and i + 1 < last:
                 quantise(i + 1)
                 passes(i + 1)
             if i + 2 < UNITS:

from contextlib import ExitStack

import concourse.mybir as mybir
from concourse.masks import make_identity

F32 = mybir.dt.float32
BF16 = mybir.dt.bfloat16
U32 = mybir.dt.uint32
U8 = mybir.dt.uint8
FP8X4 = mybir.dt.float8_e4m3fn_x4
ACT = mybir.ActivationFunctionType
ALU = mybir.AluOpType

B, C, HW = 4, 512, 1024
P = 128
PACK = 4
NPIX = 512
HALVES = HW // NPIX
UNITS = B * HALVES
FLOPS = 2 * B * C * C * HW

MANUAL = True
WS = (256, 352, 288, 336, 336, 336, 336, 448)
SPLIT = ((128, 128), (256, 96))
MULG = (1, 1, 1, 1, 1, 1, 1, 1)
STG = (2, 2, 2, 2, 2, 2, 1, 1)
VFORM = "perm"
TAIL = 2
EARLY = (0, 0, 0, 0, 0, 0, 0, 0)


def tile_gdn_kernel(tc, x, gamma, beta, out):
    nc = tc.nc
    xv = x.rearrange("b (p j) h w -> b p j (h w)", j=PACK)
    ov = out.rearrange("b (p j) h w -> b p j (h w)", j=PACK)
    gv = gamma.rearrange("(p j) c -> p j c", j=PACK)
    bv = beta.rearrange("(p j) -> p j", j=PACK)

    with ExitStack() as ctx:
        if MANUAL:
            ctx.enter_context(tc.manual_schedule())
        const = ctx.enter_context(tc.tile_pool(name="const", bufs=1))
        grp_pool = ctx.enter_context(tc.tile_pool(name="grp", bufs=4))
        q_pool = ctx.enter_context(tc.tile_pool(name="q", bufs=4))
        r_pool = ctx.enter_context(tc.tile_pool(name="r", bufs=6))
        o_pool = ctx.enter_context(tc.tile_pool(name="o", bufs=4))
        psum = ctx.enter_context(tc.psum_pool(name="psum", bufs=8))

        x0_sb = [const.tile([P, PACK, NPIX], BF16, name="x0%d" % h) for h in range(2 * HALVES)]
        x_sb = [None, None] + [const.tile([P, PACK, HW], BF16, name="x%d" % b) for b in range(2, B)]
        g_sb = const.tile([P, PACK, C], BF16, name="g_sb")
        nc.sync.dma_start(out=g_sb[:, 0:2, :], in_=gv[:, 0:2, :])
        xp = [const.tile([P, 2, PACK, NPIX // 2], BF16, name="xp%d" % u) for u in range(2)]
        for a in range(2):
            nc.sync.dma_start(out=xp[0][:, a, :, :], in_=xv[0][:, :, a * (NPIX // 2):(a + 1) * (NPIX // 2)])
        nc.sync.dma_start(out=g_sb[:, 2:4, :], in_=gv[:, 2:4, :])
        for a in range(2):
            nc.sync.dma_start(out=xp[1][:, a, :, :], in_=xv[0][:, :, NPIX + a * (NPIX // 2):NPIX + (a + 1) * (NPIX // 2)])
        for h in range(HALVES):
            nc.sync.dma_start(out=x0_sb[HALVES + h][:], in_=xv[1][:, :, h * NPIX:(h + 1) * NPIX])
        for b in range(2, B):
            nc.sync.dma_start(out=x_sb[b][:], in_=xv[b])
        beta_bf = const.tile([P, PACK], BF16, name="beta_bf")
        nc.scalar.dma_start(out=beta_bf[:], in_=bv)

        warm_in = const.tile([P, 1], F32, name="warm_in")
        warm_out = const.tile([P, 1], F32, name="warm_out")
        nc.vector.memset(warm_in[:], 1.0)
        nc.scalar.activation(out=warm_out[:], in_=warm_in[:], func=ACT.Abs_reciprocal_sqrt)

        ident = const.tile([P, P], F32, name="ident")
        make_identity(nc, ident[:])
        beta_f = const.tile([P, PACK], F32, name="beta_f")
        nc.gpsimd.tensor_copy(out=beta_f[:], in_=beta_bf[:])

        grp = {}
        codes = {}
        scales = {}
        acc = {}

        def x_unit(u):
            b, h = divmod(u, HALVES)
            if b < 2:
                return x0_sb[u][:]
            return x_sb[b][:, :, h * NPIX:(h + 1) * NPIX]

        def squares_s(u):
            ws = WS[u]
            src = x_unit(u)
            nc.scalar.activation(
                out=grp[u][:, 0:ws, :].rearrange("p (c i) t -> p c t i", i=4),
                in_=src[:, :, 0:ws].rearrange("p t (c i) -> p c t i", i=4),
                func=ACT.Square,
            )

        def squares_v(u):
            ws = WS[u]
            grp[u] = grp_pool.tile([P, NPIX, PACK], BF16, name="grp", align_bytes=64)
            src = x_unit(u)
            if VFORM == "perm":
                sv = src[:, :, ws:NPIX].rearrange("p t w -> p w t")
                dv = grp[u][:, ws:NPIX, :]
            else:
                sv = src[:, :, ws:NPIX].rearrange("p t (c i) -> p c t i", i=4)
                dv = grp[u][:, ws:NPIX, :].rearrange("p (c i) t -> p c t i", i=4)
            nc.vector.tensor_tensor(out=dv, in0=sv, in1=sv, op=ALU.mult)

        def quantise(u):
            codes[u] = q_pool.tile([P, NPIX], U32, name="codes", align_bytes=64)
            scales[u] = q_pool.tile([P, NPIX], U8, name="scales", align_bytes=64)
            nc.vector.quantize_mx(
                out=codes[u][:].bitcast(FP8X4),
                scales=scales[u][:],
                in_=grp[u][:].rearrange("p w t -> p (w t)"),
            )

        def passes(u):
            for j in range(PACK):
                acc[u, j] = psum.tile([P, NPIX], F32, name="bank")
                nc.tensor.matmul_mx(
                    out=acc[u, j][:],
                    lhsT=g_codes[:, j * P:(j + 1) * P].bitcast(FP8X4),
                    lhsT_scale=g_scales[:, j * P:(j + 1) * P],
                    rhs=codes[u][:].bitcast(FP8X4),
                    rhs_scale=scales[u][:],
                    start=True,
                    stop=True,
                )

        o_tiles = {}

        def finish(u, j_list):
            b, h = divmod(u, HALVES)
            mg, sg = MULG[u], STG[u]
            src = x_unit(u)
            if j_list[0] == 0:
                o_tiles[u] = o_pool.tile([P, PACK, NPIX], F32, name="o_sb")
            o_sb = o_tiles[u]
            r_sb = None
            for j in j_list:
                if u == UNITS - 1 and j == PACK - 1 and TAIL > 1:
                    r_sb = r_pool.tile([P, 1, NPIX], F32, name="r_sb")
                    w = NPIX // TAIL
                    for k in range(TAIL):
                        cols = slice(k * w, (k + 1) * w)
                        nc.scalar.activation(
                            out=r_sb[:, 0, cols], in_=acc[u, j][:, cols], func=ACT.Abs_reciprocal_sqrt,
                            bias=beta_f[:, j:j + 1], scale=1.0,
                        )
                        nc.vector.tensor_tensor(out=o_sb[:, j, cols], in0=src[:, j, cols], in1=r_sb[:, 0, cols], op=ALU.mult)
                        nc.sync.dma_start(out=ov[b][:, j, h * NPIX + k * w:h * NPIX + (k + 1) * w], in_=o_sb[:, j, cols])
                    continue
                if j % mg == 0:
                    r_sb = r_pool.tile([P, mg, NPIX], F32, name="r_sb")
                nc.scalar.activation(
                    out=r_sb[:, j % mg, :], in_=acc[u, j][:], func=ACT.Abs_reciprocal_sqrt,
                    bias=beta_f[:, j:j + 1], scale=1.0,
                )
                if u < 2:
                    nc.vector.tensor_tensor(
                        out=o_sb[:, j, :].rearrange("p (a w) -> p a w", a=2), in0=xp[u][:, :, j, :],
                        in1=r_sb[:, 0, :].rearrange("p (a w) -> p a w", a=2), op=ALU.mult)
                elif (j + 1) % mg == 0:
                    js = slice(j + 1 - mg, j + 1)
                    nc.vector.tensor_tensor(out=o_sb[:, js, :], in0=src[:, js, :], in1=r_sb[:], op=ALU.mult)
                if (j + 1) % sg == 0:
                    js = slice(j + 1 - sg, j + 1)
                    nc.sync.dma_start(out=ov[b][:, js, h * NPIX:(h + 1) * NPIX], in_=o_sb[:, js, :])

        g_words = g_sb[:].bitcast(F32).rearrange("p j (q u) -> p j q u", u=2)
        g_grp = const.tile([P, PACK, P, PACK], BF16, name="g_grp", align_bytes=64)
        g_grp_words = g_grp[:].bitcast(F32)
        g_codes = const.tile([P, C], U32, name="g_codes", align_bytes=64)
        g_scales = const.tile([P, C], U8, name="g_scales", align_bytes=64)
        g_t = []

        def g_transposes(half):
            g_t.append(psum.tile([P, 4, P], F32, name="bank"))
            for jj in range(2):
                for u in range(2):
                    nc.tensor.transpose(g_t[half][:, 2 * jj + u, :], g_words[:, 2 * half + jj, :, u], ident[:])

        def g_copy(half, on_scalar):
            dst = g_grp_words[:, 2 * half:2 * half + 2, :, :]
            src = g_t[half][:].rearrange("p (jj u) o -> p jj o u", u=2)
            if on_scalar:
                nc.scalar.copy(out=dst, in_=src)
            else:
                nc.vector.tensor_copy(out=dst, in_=src)

        def g_quantise(half):
            cols = slice(half * 2 * P, (half + 1) * 2 * P)
            nc.vector.quantize_mx(
                out=g_codes[:, cols].bitcast(FP8X4),
                scales=g_scales[:, cols],
                in_=g_grp[:, 2 * half:2 * half + 2, :, :].rearrange("p j o t -> p (j o t)"),
            )

        hp = NPIX // 2

        def squares_pieces(u):
            grp[u] = grp_pool.tile([P, NPIX, PACK], BF16, name="grp", align_bytes=64)
            for a in range(2):
                w0 = SPLIT[u][a]
                nc.scalar.activation(
                    out=grp[u][:, a * hp:a * hp + w0, :].rearrange("p (c i) t -> p c t i", i=4),
                    in_=xp[u][:, a, :, 0:w0].rearrange("p t (c i) -> p c t i", i=4),
                    func=ACT.Square,
                )
                if w0 < hp:
                    sv0 = xp[u][:, a, :, w0:hp].rearrange("p t w -> p w t")
                    nc.vector.tensor_tensor(out=grp[u][:, a * hp + w0:(a + 1) * hp, :], in0=sv0, in1=sv0, op=ALU.mult)

        squares_pieces(0)
        g_transposes(0)
        g_transposes(1)
        quantise(0)
        g_copy(0, True)
        g_quantise(0)
        squares_pieces(1)
        g_copy(1, False)
        quantise(1)
        g_quantise(1)
        passes(0)
        passes(1)
        last = UNITS - 1
        for i in range(UNITS):
            if 0 < i and i + 1 < last:
                quantise(i + 1)
                passes(i + 1)
            if i + 2 < UNITS:
                squares_v(i + 2)
            if i + 2 < last:
                squares_s(i + 2)
            finish(i, list(range(PACK)))
            if i + 2 == last:
                squares_s(last)
                quantise(last)
                passes(last)
